import numpy as np
import ml_dtypes


def mxq(x, axis, fmt="e4m3"):
    dtype, down = {"e4m3": (ml_dtypes.float8_e4m3fn, 7), "e5m2": (ml_dtypes.float8_e5m2, 14)}[fmt]
    v = np.moveaxis(np.asarray(x, np.float32).astype(ml_dtypes.bfloat16).astype(np.float64), axis, -1)
    blocks = v.reshape(v.shape[:-1] + (-1, 32))
    amax = np.abs(blocks).max(-1, keepdims=True)
    byte = np.maximum(np.where(amax > 0, np.frexp(amax)[1] - 1 + 127, 0) - down, 1)
    scale = np.exp2(byte - 127.0)
    codes = (blocks / scale).astype(np.float32).astype(dtype).astype(np.float64)
    return np.moveaxis((codes * scale).reshape(v.shape), -1, axis)


WIDE = False


def mx_kscale(k):
    if not WIDE:
        return np.ones(k)
    levels = np.array([10, -10, 5, -5, 0])
    a = np.random.permutation(np.resize(levels, k // 512 * 4)).reshape(k // 512, 4)
    idx = np.arange(k)
    return np.exp2(a[idx // 512, idx % 128 // 32])


BF16 = ml_dtypes.bfloat16


def bf(x):
    return np.asarray(x, np.float32).astype(BF16)


def f64(x):
    return np.asarray(x).astype(np.float64)


B, R, U, HID, G = 4096, 1024, 512, 1024, 256


def sigmoid(v):
    return 1.0 / (1.0 + np.exp(-v))


def setup_inputs():
    s = mx_kscale(R)
    return {"y_tilde": bf(np.random.standard_normal((B, R)) * s),
            "z_next": bf(np.random.standard_normal((B, R)) * s),
            "dt": bf(0.3 + 0.2 * np.random.random(1)),
            "glu_w1": bf(np.random.standard_normal((G, R)) * 1.5 / np.sqrt(R) / s),
            "glu_w2": bf(np.random.standard_normal((G, R)) / np.sqrt(R) / s),
            "glu_b1": bf(np.random.standard_normal(G) * 0.3),
            "glu_b2": bf(np.random.standard_normal(G) * 0.3)}


def reference(y_tilde, z_next, dt, glu_w1, glu_w2, glu_b1, glu_b2):
    y_next = f64(y_tilde) + f64(dt) * f64(z_next)
    yq = mxq(y_next, 1, "e4m3")
    gate = sigmoid((yq @ mxq(f64(glu_w1), 1, "e4m3").T) + f64(glu_b1))
    return gate * ((yq @ mxq(f64(glu_w2), 1, "e4m3").T) + f64(glu_b2))

@@ -1,0 +1,205 @@
+from contextlib import ExitStack
+
+import concourse.mybir as mybir
+from concourse.masks import make_identity
+
+BF16 = mybir.dt.bfloat16
+F32 = mybir.dt.float32
+U32 = mybir.dt.uint32
+U8 = mybir.dt.uint8
+FP8X4 = mybir.dt.float8_e4m3fn_x4
+ACT = mybir.ActivationFunctionType
+ALU = mybir.AluOpType
+
+P = 128
+ROWS, MODES, UNITS = 4096, 1024, 256
+K_PASS = 4 * P
+PASSES = MODES // K_PASS
+ROW_GROUPS = 4
+CHUNK_ROWS = P * ROW_GROUPS
+CHUNKS = ROWS // CHUNK_ROWS
+PAIRS = ROW_GROUPS // 2
+UNIT_TILES = UNITS // P
+LOADS_AHEAD = 3
+
+FLOPS = 2 * ROWS * MODES * 2 * UNITS
+
+
+def turn_and_group(nc, turned_pool, ident, row_words, grouped_words, pair):
+    columns = slice(2 * pair * P, 2 * (pair + 1) * P)
+    for g in range(PASSES):
+        turned = turned_pool.tile([P, 2, 2, P], F32, tag="turned")
+        for jj in range(2):
+            for u in range(2):
+                first_word = (2 * g + u) * P
+                nc.tensor.transpose(
+                    turned[:, jj, u, :],
+                    row_words[:, 2 * pair + jj, first_word : first_word + P],
+                    ident[:],
+                )
+        nc.scalar.copy(
+            out=grouped_words[:, g, columns, :].rearrange("p (j q) u -> p j q u", j=2),
+            in_=turned[:].rearrange("p j u q -> p j q u"),
+        )
+
+
+def quantise(nc, grouped, codes, scales):
+    for g in range(PASSES):
+        nc.vector.quantize_mx(
+            out=codes[:, g, :].bitcast(FP8X4),
+            scales=scales[:, g, :],
+            in_=grouped[:, g, :, :].rearrange("p c t -> p (c t)"),
+        )
+
+
+def tile_instrumentedlocmblock_pb_t_kernel(
+    tc, y_tilde, z_next, dt, glu_w1, glu_w2, glu_b1, glu_b2, out
+):
+    nc = tc.nc
+    y_chunks = y_tilde.rearrange("(c q j) k -> c q j k", q=P, j=ROW_GROUPS)
+    z_chunks = z_next.rearrange("(c q j) k -> c q j k", q=P, j=ROW_GROUPS)
+    out_chunks = out.rearrange("(c q j) n -> c q j n", q=P, j=ROW_GROUPS)
+
+    with ExitStack() as ctx:
+        const = ctx.enter_context(tc.tile_pool(name="const", bufs=1))
+        loads = ctx.enter_context(tc.tile_pool(name="loads", bufs=LOADS_AHEAD + 1))
+        work = ctx.enter_context(tc.tile_pool(name="work", bufs=2))
+        turned_pool = ctx.enter_context(tc.psum_pool(name="turned", bufs=2))
+        sums_pool = ctx.enter_context(tc.psum_pool(name="sums", bufs=2 * UNIT_TILES))
+        back_pool = ctx.enter_context(tc.psum_pool(name="back", bufs=2))
+        ctx.enter_context(tc.manual_schedule())
+
+        loaded = {}
+        grouped_of = {}
+
+        def load(c):
+            y_rows = loads.tile([P, ROW_GROUPS, MODES], BF16)
+            z_rows = loads.tile([P, ROW_GROUPS, MODES], BF16)
+            for pair in range(PAIRS):
+                groups = slice(2 * pair, 2 * pair + 2)
+                nc.sync.dma_start(out=y_rows[:, groups, :], in_=y_chunks[c][:, groups, :])
+                nc.sync.dma_start(out=z_rows[:, groups, :], in_=z_chunks[c][:, groups, :])
+            loaded[c] = (y_rows, z_rows)
+
+        def add_and_turn(c):
+            y_rows, z_rows = loaded[c]
+            y_next = work.tile([P, ROW_GROUPS, MODES], BF16)
+            grouped = work.tile([P, PASSES, CHUNK_ROWS, 4], BF16, align_bytes=64)
+            for pair in range(PAIRS):
+                groups = slice(2 * pair, 2 * pair + 2)
+                nc.vector.scalar_tensor_tensor(
+                    out=y_next[:, groups, :],
+                    in0=z_rows[:, groups, :],
+                    scalar=dt_col[:, 0:1],
+                    in1=y_rows[:, groups, :],
+                    op0=ALU.mult,
+                    op1=ALU.add,
+                )
+                turn_and_group(
+                    nc, turned_pool, ident, y_next[:].bitcast(F32), grouped[:].bitcast(F32), pair
+                )
+            grouped_of[c] = grouped
+
+        def quantise_and_multiply(c):
+            y_codes = work.tile([P, PASSES, CHUNK_ROWS], U32, align_bytes=64)
+            y_scales = work.tile([P, PASSES, CHUNK_ROWS], U8, align_bytes=64)
+            quantise(nc, grouped_of[c], y_codes, y_scales)
+            halves = []
+            for h in range(UNIT_TILES):
+                gate_sum = sums_pool.tile([P, CHUNK_ROWS], F32, tag="sum")
+                value_sum = sums_pool.tile([P, CHUNK_ROWS], F32, tag="sum")
+                for acc, unit_tile in ((gate_sum, h), (value_sum, UNIT_TILES + h)):
+                    units = slice(unit_tile * P, (unit_tile + 1) * P)
+                    for g in range(PASSES):
+                        nc.tensor.matmul_mx(
+                            out=acc[:],
+                            lhsT=w_codes[:, g, units].bitcast(FP8X4),
+                            lhsT_scale=w_scales[:, g, units],
+                            rhs=y_codes[:, g, :].bitcast(FP8X4),
+                            rhs_scale=y_scales[:, g, :],
+                            start=(g == 0),
+                            stop=(g == PASSES - 1),
+                        )
+                gate = work.tile([P, CHUNK_ROWS], F32)
+                nc.scalar.activation(
+                    out=gate[:], in_=gate_sum[:], func=ACT.Sigmoid, bias=bias_col[:, h : h + 1], scale=1.0
+                )
+                halves.append((gate, value_sum))
+            return halves
+
+        def gate_and_store(c, halves):
+            product = work.tile([P, UNIT_TILES, CHUNK_ROWS], F32)
+            for h in range(UNIT_TILES):
+                gate, value_sum = halves[h]
+                nc.vector.scalar_tensor_tensor(
+                    out=product[:, h, :],
+                    in0=value_sum[:],
+                    scalar=bias_col[:, UNIT_TILES + h : UNIT_TILES + h + 1],
+                    in1=gate[:],
+                    op0=ALU.add,
+                    op1=ALU.mult,
+                )
+            result = work.tile([P, ROW_GROUPS, UNITS], F32)
+            for pair in range(PAIRS):
+                back = back_pool.tile([P, 2, UNITS], F32)
+                for jj in range(2):
+                    rows = slice((2 * pair + jj) * P, (2 * pair + jj + 1) * P)
+                    for h in range(UNIT_TILES):
+                        nc.tensor.transpose(
+                            back[:, jj, h * P : (h + 1) * P], product[:, h, rows], ident[:]
+                        )
+                nc.scalar.copy(out=result[:, 2 * pair : 2 * pair + 2, :], in_=back[:])
+            nc.sync.dma_start(out=out_chunks[c], in_=result[:])
+
+        ident = const.tile([P, P], F32)
+        make_identity(nc, ident[:])
+
+        dt_bf16 = const.tile([P, 1], BF16)
+        nc.scalar.dma_start(out=dt_bf16[:], in_=dt.partition_broadcast(P))
+        bias_bf16 = const.tile([2 * UNIT_TILES, P], BF16)
+        nc.scalar.dma_start(
+            out=bias_bf16[0:UNIT_TILES, :], in_=glu_b1.rearrange("(h n) -> h n", n=P)
+        )
+        nc.scalar.dma_start(
+            out=bias_bf16[UNIT_TILES : 2 * UNIT_TILES, :], in_=glu_b2.rearrange("(h n) -> h n", n=P)
+        )
+
+        load(0)
+        w_rows = const.tile([P, 2 * UNIT_TILES, MODES], BF16)
+        nc.sync.dma_start(
+            out=w_rows[:, 0:UNIT_TILES, :], in_=glu_w1.rearrange("(h q) k -> q h k", q=P)
+        )
+        nc.sync.dma_start(
+            out=w_rows[:, UNIT_TILES : 2 * UNIT_TILES, :], in_=glu_w2.rearrange("(h q) k -> q h k", q=P)
+        )
+        for c in range(1, LOADS_AHEAD):
+            load(c)
+
+        dt_col = const.tile([P, 1], F32)
+        nc.vector.tensor_copy(out=dt_col[:], in_=dt_bf16[:])
+        bias_rows = const.tile([P, P], F32)
+        nc.vector.memset(bias_rows[:], 0.0)
+        nc.vector.tensor_copy(out=bias_rows[0 : 2 * UNIT_TILES, :], in_=bias_bf16[:])
+        bias_turned = turned_pool.tile([P, 2, 2, P], F32, tag="turned")
+        nc.tensor.transpose(bias_turned[:, 0, 0, :], bias_rows[:], ident[:])
+        bias_col = const.tile([P, 2 * UNIT_TILES], F32)
+        nc.scalar.copy(out=bias_col[:], in_=bias_turned[:, 0, 0, 0 : 2 * UNIT_TILES])
+
+        add_and_turn(0)
+
+        w_grouped = work.tile([P, PASSES, CHUNK_ROWS, 4], BF16, align_bytes=64, tag="grouped")
+        for pair in range(PAIRS):
+            turn_and_group(
+                nc, turned_pool, ident, w_rows[:].bitcast(F32), w_grouped[:].bitcast(F32), pair
+            )
+        w_codes = const.tile([P, PASSES, CHUNK_ROWS], U32, align_bytes=64)
+        w_scales = const.tile([P, PASSES, CHUNK_ROWS], U8, align_bytes=64)
+        quantise(nc, w_grouped, w_codes, w_scales)
+
+        for c in range(CHUNKS):
+            if c + LOADS_AHEAD < CHUNKS:
+                load(c + LOADS_AHEAD)
+            halves = quantise_and_multiply(c)
+            if c + 1 < CHUNKS:
+                add_and_turn(c + 1)
+            gate_and_store(c, halves)

@@ -20,7 +20,7 @@ CHUNK_ROWS = P * ROW_GROUPS
 CHUNKS = ROWS // CHUNK_ROWS
 PAIRS = ROW_GROUPS // 2
 UNIT_TILES = UNITS // P
-LOADS_AHEAD = 3
+CHUNKS_IN_SBUF = 4
 
 FLOPS = 2 * ROWS * MODES * 2 * UNITS
 
@@ -44,12 +44,11 @@ def turn_and_group(nc, turned_pool, ident, row_words, grouped_words, pair):
 
 
 def quantise(nc, grouped, codes, scales):
-    for g in range(PASSES):
-        nc.vector.quantize_mx(
-            out=codes[:, g, :].bitcast(FP8X4),
-            scales=scales[:, g, :],
-            in_=grouped[:, g, :, :].rearrange("p c t -> p (c t)"),
-        )
+    nc.vector.quantize_mx(
+        out=codes[:].rearrange("p g c -> p (g c)").bitcast(FP8X4),
+        scales=scales[:].rearrange("p g c -> p (g c)"),
+        in_=grouped[:].rearrange("p g c t -> p (g c t)"),
+    )
 
 
 def tile_instrumentedlocmblock_pb_t_kernel(
@@ -62,7 +61,7 @@ def tile_instrumentedlocmblock_pb_t_kernel(
 
     with ExitStack() as ctx:
         const = ctx.enter_context(tc.tile_pool(name="const", bufs=1))
-        loads = ctx.enter_context(tc.tile_pool(name="loads", bufs=LOADS_AHEAD + 1))
+        loads = ctx.enter_context(tc.tile_pool(name="loads", bufs=CHUNKS_IN_SBUF))
         work = ctx.enter_context(tc.tile_pool(name="work", bufs=2))
         turned_pool = ctx.enter_context(tc.psum_pool(name="turned", bufs=2))
         sums_pool = ctx.enter_context(tc.psum_pool(name="sums", bufs=2 * UNIT_TILES))
@@ -84,7 +83,7 @@ def tile_instrumentedlocmblock_pb_t_kernel(
         def add_and_turn(c):
             y_rows, z_rows = loaded[c]
             y_next = work.tile([P, ROW_GROUPS, MODES], BF16)
-            grouped = work.tile([P, PASSES, CHUNK_ROWS, 4], BF16, align_bytes=64)
+            grouped = work.tile([P, PASSES, CHUNK_ROWS, 4], BF16, align_bytes=64, bufs=3)
             for pair in range(PAIRS):
                 groups = slice(2 * pair, 2 * pair + 2)
                 nc.vector.scalar_tensor_tensor(
@@ -120,7 +119,7 @@ def tile_instrumentedlocmblock_pb_t_kernel(
                             start=(g == 0),
                             stop=(g == PASSES - 1),
                         )
-                gate = work.tile([P, CHUNK_ROWS], F32)
+                gate = work.tile([P, CHUNK_ROWS], F32, bufs=2 * UNIT_TILES)
                 nc.scalar.activation(
                     out=gate[:], in_=gate_sum[:], func=ACT.Sigmoid, bias=bias_col[:, h : h + 1], scale=1.0
                 )
@@ -129,6 +128,10 @@ def tile_instrumentedlocmblock_pb_t_kernel(
 
         def gate_and_store(c, halves):
             product = work.tile([P, UNIT_TILES, CHUNK_ROWS], F32)
+            backs = [
+                back_pool.tile([P, 2, UNITS], F32, name="back%d" % pair, tag="back")
+                for pair in range(PAIRS)
+            ]
             for h in range(UNIT_TILES):
                 gate, value_sum = halves[h]
                 nc.vector.scalar_tensor_tensor(
@@ -139,17 +142,17 @@ def tile_instrumentedlocmblock_pb_t_kernel(
                     op0=ALU.add,
                     op1=ALU.mult,
                 )
+                for j in range(ROW_GROUPS):
+                    nc.tensor.transpose(
+                        backs[j // 2][:, j % 2, h * P : (h + 1) * P],
+                        product[:, h, j * P : (j + 1) * P],
+                        ident[:],
+                    )
             result = work.tile([P, ROW_GROUPS, UNITS], F32)
             for pair in range(PAIRS):
-                back = back_pool.tile([P, 2, UNITS], F32)
-                for jj in range(2):
-                    rows = slice((2 * pair + jj) * P, (2 * pair + jj + 1) * P)
-                    for h in range(UNIT_TILES):
-                        nc.tensor.transpose(
-                            back[:, jj, h * P : (h + 1) * P], product[:, h, rows], ident[:]
-                        )
-                nc.scalar.copy(out=result[:, 2 * pair : 2 * pair + 2, :], in_=back[:])
-            nc.sync.dma_start(out=out_chunks[c], in_=result[:])
+                groups = slice(2 * pair, 2 * pair + 2)
+                nc.scalar.copy(out=result[:, groups, :], in_=backs[pair][:])
+                nc.sync.dma_start(out=out_chunks[c][:, groups, :], in_=result[:, groups, :])
 
         ident = const.tile([P, P], F32)
         make_identity(nc, ident[:])
@@ -172,11 +175,14 @@ def tile_instrumentedlocmblock_pb_t_kernel(
         nc.sync.dma_start(
             out=w_rows[:, UNIT_TILES : 2 * UNIT_TILES, :], in_=glu_w2.rearrange("(h q) k -> q h k", q=P)
         )
-        for c in range(1, LOADS_AHEAD):
+        for c in range(1, CHUNKS_IN_SBUF):
             load(c)
 
         dt_col = const.tile([P, 1], F32)
         nc.vector.tensor_copy(out=dt_col[:], in_=dt_bf16[:])
+
+        add_and_turn(0)
+
         bias_rows = const.tile([P, P], F32)
         nc.vector.memset(bias_rows[:], 0.0)
         nc.vector.tensor_copy(out=bias_rows[0 : 2 * UNIT_TILES, :], in_=bias_bf16[:])
@@ -185,21 +191,23 @@ def tile_instrumentedlocmblock_pb_t_kernel(
         bias_col = const.tile([P, 2 * UNIT_TILES], F32)
         nc.scalar.copy(out=bias_col[:], in_=bias_turned[:, 0, 0, 0 : 2 * UNIT_TILES])
 
-        add_and_turn(0)
-
-        w_grouped = work.tile([P, PASSES, CHUNK_ROWS, 4], BF16, align_bytes=64, tag="grouped")
+        w_grouped = work.tile([P, PASSES, CHUNK_ROWS, 4], BF16, align_bytes=64, tag="grouped", bufs=3)
         for pair in range(PAIRS):
             turn_and_group(
                 nc, turned_pool, ident, w_rows[:].bitcast(F32), w_grouped[:].bitcast(F32), pair
             )
+        add_and_turn(1)
         w_codes = const.tile([P, PASSES, CHUNK_ROWS], U32, align_bytes=64)
         w_scales = const.tile([P, PASSES, CHUNK_ROWS], U8, align_bytes=64)
         quantise(nc, w_grouped, w_codes, w_scales)
 
-        for c in range(CHUNKS):
-            if c + LOADS_AHEAD < CHUNKS:
-                load(c + LOADS_AHEAD)
-            halves = quantise_and_multiply(c)
-            if c + 1 < CHUNKS:
-                add_and_turn(c + 1)
-            gate_and_store(c, halves)
+        halves_of = {}
+        for c in range(CHUNKS + 1):
+            if c + CHUNKS_IN_SBUF < CHUNKS:
+                load(c + CHUNKS_IN_SBUF)
+            if c < CHUNKS:
+                halves_of[c] = quantise_and_multiply(c)
+            if c >= 1:
+                gate_and_store(c - 1, halves_of[c - 1])
+            if c + 2 < CHUNKS:
+                add_and_turn(c + 2)

@@ -21,6 +21,7 @@ CHUNKS = ROWS // CHUNK_ROWS
 PAIRS = ROW_GROUPS // 2
 UNIT_TILES = UNITS // P
 CHUNKS_IN_SBUF = 4
+DT_ROW = 32
 
 FLOPS = 2 * ROWS * MODES * 2 * UNITS
 
@@ -157,14 +158,13 @@ def tile_instrumentedlocmblock_pb_t_kernel(
         ident = const.tile([P, P], F32)
         make_identity(nc, ident[:])
 
-        dt_bf16 = const.tile([P, 1], BF16)
-        nc.scalar.dma_start(out=dt_bf16[:], in_=dt.partition_broadcast(P))
-        bias_bf16 = const.tile([2 * UNIT_TILES, P], BF16)
-        nc.scalar.dma_start(
-            out=bias_bf16[0:UNIT_TILES, :], in_=glu_b1.rearrange("(h n) -> h n", n=P)
+        small_rows = const.tile([DT_ROW + 1, P], BF16)
+        nc.sync.dma_start(out=small_rows[DT_ROW : DT_ROW + 1, 0:1], in_=dt.unsqueeze(0))
+        nc.sync.dma_start(
+            out=small_rows[0:UNIT_TILES, :], in_=glu_b1.rearrange("(h n) -> h n", n=P)
         )
-        nc.scalar.dma_start(
-            out=bias_bf16[UNIT_TILES : 2 * UNIT_TILES, :], in_=glu_b2.rearrange("(h n) -> h n", n=P)
+        nc.sync.dma_start(
+            out=small_rows[UNIT_TILES : 2 * UNIT_TILES, :], in_=glu_b2.rearrange("(h n) -> h n", n=P)
         )
 
         load(0)
@@ -178,18 +178,23 @@ def tile_instrumentedlocmblock_pb_t_kernel(
         for c in range(1, CHUNKS_IN_SBUF):
             load(c)
 
-        dt_col = const.tile([P, 1], F32)
-        nc.vector.tensor_copy(out=dt_col[:], in_=dt_bf16[:])
+        wide_rows = const.tile([P, P], F32)
+        nc.vector.memset(wide_rows[:], 0.0)
+        nc.vector.tensor_copy(
+            out=wide_rows[0 : 2 * UNIT_TILES, :], in_=small_rows[0 : 2 * UNIT_TILES, :]
+        )
+        nc.vector.tensor_copy(
+            out=wide_rows[DT_ROW : DT_ROW + 1, :],
+            in_=small_rows[DT_ROW : DT_ROW + 1, 0:1].to_broadcast([1, P]),
+        )
+        rows_turned = turned_pool.tile([P, 2, 2, P], F32, tag="turned")
+        nc.tensor.transpose(rows_turned[:, 0, 0, :], wide_rows[:], ident[:])
+        per_partition = const.tile([P, DT_ROW + 1], F32)
+        nc.scalar.copy(out=per_partition[:], in_=rows_turned[:, 0, 0, 0 : DT_ROW + 1])
+        bias_col = per_partition[:, 0 : 2 * UNIT_TILES]
+        dt_col = per_partition[:, DT_ROW : DT_ROW + 1]
 
         add_and_turn(0)
-
-        bias_rows = const.tile([P, P], F32)
-        nc.vector.memset(bias_rows[:], 0.0)
-        nc.vector.tensor_copy(out=bias_rows[0 : 2 * UNIT_TILES, :], in_=bias_bf16[:])
-        bias_turned = turned_pool.tile([P, 2, 2, P], F32, tag="turned")
-        nc.tensor.transpose(bias_turned[:, 0, 0, :], bias_rows[:], ident[:])
-        bias_col = const.tile([P, 2 * UNIT_TILES], F32)
-        nc.scalar.copy(out=bias_col[:], in_=bias_turned[:, 0, 0, 0 : 2 * UNIT_TILES])
 
         w_grouped = work.tile([P, PASSES, CHUNK_ROWS, 4], BF16, align_bytes=64, tag="grouped", bufs=3)
         for pair in range(PAIRS):

@@ -12,36 +12,49 @@ ACT = mybir.ActivationFunctionType
 ALU = mybir.AluOpType
 
 P = 128
+HALF = P // 2
 ROWS, MODES, UNITS = 4096, 1024, 256
 K_PASS = 4 * P
 PASSES = MODES // K_PASS
 ROW_GROUPS = 4
+VECTOR_GROUPS = 3
+VECTOR_PIECES = ((0, 2), (2, VECTOR_GROUPS))
 CHUNK_ROWS = P * ROW_GROUPS
 CHUNKS = ROWS // CHUNK_ROWS
-PAIRS = ROW_GROUPS // 2
 UNIT_TILES = UNITS // P
 CHUNKS_IN_SBUF = 4
-DT_ROW = 32
 
 FLOPS = 2 * ROWS * MODES * 2 * UNITS
 
 
-def turn_and_group(nc, turned_pool, ident, row_words, grouped_words, pair):
-    columns = slice(2 * pair * P, 2 * (pair + 1) * P)
+def turn_and_group(nc, turned_pool, ident, row_words, grouped_words, j):
+    turned = turned_pool.tile([P, PASSES, 2, P], F32, tag="turned")
     for g in range(PASSES):
-        turned = turned_pool.tile([P, 2, 2, P], F32, tag="turned")
-        for jj in range(2):
-            for u in range(2):
-                first_word = (2 * g + u) * P
-                nc.tensor.transpose(
-                    turned[:, jj, u, :],
-                    row_words[:, 2 * pair + jj, first_word : first_word + P],
-                    ident[:],
+        for u in range(2):
+            first_word = (2 * g + u) * P
+            nc.tensor.transpose(
+                turned[:, g, u, :], row_words[:, j, first_word : first_word + P], ident[:]
+            )
+    nc.scalar.copy(
+        out=grouped_words[:, :, j * P : (j + 1) * P, :],
+        in_=turned[:].rearrange("p g u q -> p g q u"),
+    )
+
+
+def add_and_group(nc, turned_pool, one_and_dt, stacked, grouped, j):
+    for g in range(PASSES):
+        summed = turned_pool.tile([P, P, 4], F32, tag="turned")
+        for s in range(2):
+            for t in range(4):
+                first_k = K_PASS * g + 2 * P * (t // 2) + t % 2
+                nc.tensor.matmul(
+                    out=summed[:, s * HALF : (s + 1) * HALF, t],
+                    lhsT=stacked[:, s, first_k : first_k + 2 * P - 1 : 2],
+                    rhs=one_and_dt[:],
+                    start=True,
+                    stop=True,
                 )
-        nc.scalar.copy(
-            out=grouped_words[:, g, columns, :].rearrange("p (j q) u -> p j q u", j=2),
-            in_=turned[:].rearrange("p j u q -> p j q u"),
-        )
+        nc.scalar.copy(out=grouped[:, g, j * P : (j + 1) * P, :], in_=summed[:])
 
 
 def quantise(nc, grouped, codes, scales):
@@ -73,37 +86,49 @@ def tile_instrumentedlocmblock_pb_t_kernel(
         grouped_of = {}
 
         def load(c):
-            y_rows = loads.tile([P, ROW_GROUPS, MODES], BF16)
-            z_rows = loads.tile([P, ROW_GROUPS, MODES], BF16)
-            for pair in range(PAIRS):
-                groups = slice(2 * pair, 2 * pair + 2)
-                nc.sync.dma_start(out=y_rows[:, groups, :], in_=y_chunks[c][:, groups, :])
-                nc.sync.dma_start(out=z_rows[:, groups, :], in_=z_chunks[c][:, groups, :])
-            loaded[c] = (y_rows, z_rows)
+            stacked = loads.tile([P, 2, MODES], BF16)
+            for first_partition, chunks in ((0, y_chunks), (1, z_chunks)):
+                nc.sync.dma_start(
+                    out=stacked[first_partition:P:2, :, :],
+                    in_=chunks[c][:, VECTOR_GROUPS, :].rearrange("(s r) k -> r s k", s=2),
+                )
+            y_rows = loads.tile([P, VECTOR_GROUPS, MODES], BF16)
+            z_rows = loads.tile([P, VECTOR_GROUPS, MODES], BF16)
+            for first, last in VECTOR_PIECES:
+                nc.sync.dma_start(out=y_rows[:, first:last, :], in_=y_chunks[c][:, first:last, :])
+                nc.sync.dma_start(out=z_rows[:, first:last, :], in_=z_chunks[c][:, first:last, :])
+            loaded[c] = (y_rows, z_rows, stacked)
 
-        def add_and_turn(c):
-            y_rows, z_rows = loaded[c]
-            y_next = work.tile([P, ROW_GROUPS, MODES], BF16)
-            grouped = work.tile([P, PASSES, CHUNK_ROWS, 4], BF16, align_bytes=64, bufs=3)
-            for pair in range(PAIRS):
-                groups = slice(2 * pair, 2 * pair + 2)
+        def tensor_add(c):
+            stacked = loaded[c][2]
+            grouped = work.tile([P, PASSES, CHUNK_ROWS, 4], BF16, align_bytes=64)
+            add_and_group(nc, turned_pool, one_and_dt, stacked, grouped, VECTOR_GROUPS)
+            grouped_of[c] = grouped
+
+        def vector_add_and_turn(c):
+            y_rows, z_rows = loaded[c][0:2]
+            y_next = work.tile([P, VECTOR_GROUPS, MODES], BF16)
+            for first, last in VECTOR_PIECES:
                 nc.vector.scalar_tensor_tensor(
-                    out=y_next[:, groups, :],
-                    in0=z_rows[:, groups, :],
+                    out=y_next[:, first:last, :],
+                    in0=z_rows[:, first:last, :],
                     scalar=dt_col[:, 0:1],
-                    in1=y_rows[:, groups, :],
+                    in1=y_rows[:, first:last, :],
                     op0=ALU.mult,
                     op1=ALU.add,
                 )
-                turn_and_group(
-                    nc, turned_pool, ident, y_next[:].bitcast(F32), grouped[:].bitcast(F32), pair
-                )
-            grouped_of[c] = grouped
+                for j in range(first, last):
+                    turn_and_group(
+                        nc, turned_pool, ident, y_next[:].bitcast(F32), grouped_of[c][:].bitcast(F32), j
+                    )
 
-        def quantise_and_multiply(c):
+        def quantise_chunk(c):
             y_codes = work.tile([P, PASSES, CHUNK_ROWS], U32, align_bytes=64)
             y_scales = work.tile([P, PASSES, CHUNK_ROWS], U8, align_bytes=64)
             quantise(nc, grouped_of[c], y_codes, y_scales)
+            return y_codes, y_scales
+
+        def multiply(y_codes, y_scales):
             halves = []
             for h in range(UNIT_TILES):
                 gate_sum = sums_pool.tile([P, CHUNK_ROWS], F32, tag="sum")
@@ -131,7 +156,7 @@ def tile_instrumentedlocmblock_pb_t_kernel(
             product = work.tile([P, UNIT_TILES, CHUNK_ROWS], F32)
             backs = [
                 back_pool.tile([P, 2, UNITS], F32, name="back%d" % pair, tag="back")
-                for pair in range(PAIRS)
+                for pair in range(ROW_GROUPS // 2)
             ]
             for h in range(UNIT_TILES):
                 gate, value_sum = halves[h]
@@ -150,7 +175,7 @@ def tile_instrumentedlocmblock_pb_t_kernel(
                         ident[:],
                     )
             result = work.tile([P, ROW_GROUPS, UNITS], F32)
-            for pair in range(PAIRS):
+            for pair in range(ROW_GROUPS // 2):
                 groups = slice(2 * pair, 2 * pair + 2)
                 nc.scalar.copy(out=result[:, groups, :], in_=backs[pair][:])
                 nc.sync.dma_start(out=out_chunks[c][:, groups, :], in_=result[:, groups, :])
@@ -158,16 +183,18 @@ def tile_instrumentedlocmblock_pb_t_kernel(
         ident = const.tile([P, P], F32)
         make_identity(nc, ident[:])
 
-        small_rows = const.tile([DT_ROW + 1, P], BF16)
-        nc.sync.dma_start(out=small_rows[DT_ROW : DT_ROW + 1, 0:1], in_=dt.unsqueeze(0))
-        nc.sync.dma_start(
-            out=small_rows[0:UNIT_TILES, :], in_=glu_b1.rearrange("(h n) -> h n", n=P)
+        dt_bf16 = const.tile([P, 1], BF16)
+        nc.scalar.dma_start(out=dt_bf16[:], in_=dt.partition_broadcast(P))
+        bias_bf16 = const.tile([2 * UNIT_TILES, P], BF16)
+        nc.scalar.dma_start(
+            out=bias_bf16[0:UNIT_TILES, :], in_=glu_b1.rearrange("(h n) -> h n", n=P)
         )
-        nc.sync.dma_start(
-            out=small_rows[UNIT_TILES : 2 * UNIT_TILES, :], in_=glu_b2.rearrange("(h n) -> h n", n=P)
+        nc.scalar.dma_start(
+            out=bias_bf16[UNIT_TILES : 2 * UNIT_TILES, :], in_=glu_b2.rearrange("(h n) -> h n", n=P)
         )
+        table_warmer = const.tile([P, 1], F32)
+        nc.scalar.activation(out=table_warmer[:], in_=ident[:, 0:1], func=ACT.Sigmoid)
 
-        load(0)
         w_rows = const.tile([P, 2 * UNIT_TILES, MODES], BF16)
         nc.sync.dma_start(
             out=w_rows[:, 0:UNIT_TILES, :], in_=glu_w1.rearrange("(h q) k -> q h k", q=P)
@@ -175,44 +202,48 @@ def tile_instrumentedlocmblock_pb_t_kernel(
         nc.sync.dma_start(
             out=w_rows[:, UNIT_TILES : 2 * UNIT_TILES, :], in_=glu_w2.rearrange("(h q) k -> q h k", q=P)
         )
-        for c in range(1, CHUNKS_IN_SBUF):
+        for c in range(CHUNKS_IN_SBUF):
             load(c)
 
-        wide_rows = const.tile([P, P], F32)
-        nc.vector.memset(wide_rows[:], 0.0)
-        nc.vector.tensor_copy(
-            out=wide_rows[0 : 2 * UNIT_TILES, :], in_=small_rows[0 : 2 * UNIT_TILES, :]
+        dt_col = const.tile([P, 1], F32)
+        nc.vector.tensor_copy(out=dt_col[:], in_=dt_bf16[:])
+        one_and_dt = const.tile([P, HALF], BF16)
+        nc.vector.scalar_tensor_tensor(
+            out=one_and_dt[:],
+            in0=ident[:, 1:P:2],
+            scalar=dt_col[:, 0:1],
+            in1=ident[:, 0:P:2],
+            op0=ALU.mult,
+            op1=ALU.add,
         )
-        nc.vector.tensor_copy(
-            out=wide_rows[DT_ROW : DT_ROW + 1, :],
-            in_=small_rows[DT_ROW : DT_ROW + 1, 0:1].to_broadcast([1, P]),
-        )
-        rows_turned = turned_pool.tile([P, 2, 2, P], F32, tag="turned")
-        nc.tensor.transpose(rows_turned[:, 0, 0, :], wide_rows[:], ident[:])
-        per_partition = const.tile([P, DT_ROW + 1], F32)
-        nc.scalar.copy(out=per_partition[:], in_=rows_turned[:, 0, 0, 0 : DT_ROW + 1])
-        bias_col = per_partition[:, 0 : 2 * UNIT_TILES]
-        dt_col = per_partition[:, DT_ROW : DT_ROW + 1]
 
-        add_and_turn(0)
+        bias_rows = const.tile([P, P], F32)
+        nc.vector.memset(bias_rows[:], 0.0)
+        nc.vector.tensor_copy(out=bias_rows[0 : 2 * UNIT_TILES, :], in_=bias_bf16[:])
+        bias_turned = turned_pool.tile([P, PASSES, 2, P], F32, tag="turned")
+        nc.tensor.transpose(bias_turned[:, 0, 0, :], bias_rows[:], ident[:])
+        bias_col = const.tile([P, 2 * UNIT_TILES], F32)
+        nc.scalar.copy(out=bias_col[:], in_=bias_turned[:, 0, 0, 0 : 2 * UNIT_TILES])
 
-        w_grouped = work.tile([P, PASSES, CHUNK_ROWS, 4], BF16, align_bytes=64, tag="grouped", bufs=3)
-        for pair in range(PAIRS):
+        w_grouped = const.tile([P, PASSES, CHUNK_ROWS, 4], BF16, align_bytes=64)
+        for unit_tile in range(2 * UNIT_TILES):
             turn_and_group(
-                nc, turned_pool, ident, w_rows[:].bitcast(F32), w_grouped[:].bitcast(F32), pair
+                nc, turned_pool, ident, w_rows[:].bitcast(F32), w_grouped[:].bitcast(F32), unit_tile
             )
-        add_and_turn(1)
+
+        tensor_add(0)
+        vector_add_and_turn(0)
         w_codes = const.tile([P, PASSES, CHUNK_ROWS], U32, align_bytes=64)
         w_scales = const.tile([P, PASSES, CHUNK_ROWS], U8, align_bytes=64)
         quantise(nc, w_grouped, w_codes, w_scales)
 
-        halves_of = {}
-        for c in range(CHUNKS + 1):
+        for c in range(CHUNKS):
             if c + CHUNKS_IN_SBUF < CHUNKS:
                 load(c + CHUNKS_IN_SBUF)
-            if c < CHUNKS:
-                halves_of[c] = quantise_and_multiply(c)
-            if c >= 1:
-                gate_and_store(c - 1, halves_of[c - 1])
-            if c + 2 < CHUNKS:
-                add_and_turn(c + 2)
+            y_codes, y_scales = quantise_chunk(c)
+            if c + 1 < CHUNKS:
+                tensor_add(c + 1)
+            halves = multiply(y_codes, y_scales)
+            if c + 1 < CHUNKS:
+                vector_add_and_turn(c + 1)
+            gate_and_store(c, halves)

from contextlib import ExitStack

import concourse.mybir as mybir
from concourse.masks import make_identity

BF16 = mybir.dt.bfloat16
F32 = mybir.dt.float32
U32 = mybir.dt.uint32
U8 = mybir.dt.uint8
FP8X4 = mybir.dt.float8_e4m3fn_x4
ACT = mybir.ActivationFunctionType
ALU = mybir.AluOpType

P = 128
HALF = P // 2
ROWS, MODES, UNITS = 4096, 1024, 256
K_PASS = 4 * P
PASSES = MODES // K_PASS
ROW_GROUPS = 4
VECTOR_GROUPS = 3
VECTOR_PIECES = ((0, 2), (2, VECTOR_GROUPS))
CHUNK_ROWS = P * ROW_GROUPS
CHUNKS = ROWS // CHUNK_ROWS
UNIT_TILES = UNITS // P
CHUNKS_IN_SBUF = 4

FLOPS = 2 * ROWS * MODES * 2 * UNITS


def turn_and_group(nc, turned_pool, ident, row_words, grouped_words, j):
    turned = turned_pool.tile([P, PASSES, 2, P], F32, tag="turned")
    for g in range(PASSES):
        for u in range(2):
            first_word = (2 * g + u) * P
            nc.tensor.transpose(
                turned[:, g, u, :], row_words[:, j, first_word : first_word + P], ident[:]
            )
    nc.scalar.copy(
        out=grouped_words[:, :, j * P : (j + 1) * P, :],
        in_=turned[:].rearrange("p g u q -> p g q u"),
    )


def add_and_group(nc, turned_pool, one_and_dt, stacked, grouped, j):
    for g in range(PASSES):
        summed = turned_pool.tile([P, P, 4], F32, tag="turned")
        for s in range(2):
            for t in range(4):
                first_k = K_PASS * g + 2 * P * (t // 2) + t % 2
                nc.tensor.matmul(
                    out=summed[:, s * HALF : (s + 1) * HALF, t],
                    lhsT=stacked[:, s, first_k : first_k + 2 * P - 1 : 2],
                    rhs=one_and_dt[:],
                    start=True,
                    stop=True,
                )
        nc.scalar.copy(out=grouped[:, g, j * P : (j + 1) * P, :], in_=summed[:])


def quantise(nc, grouped, codes, scales):
    nc.vector.quantize_mx(
        out=codes[:].rearrange("p g c -> p (g c)").bitcast(FP8X4),
        scales=scales[:].rearrange("p g c -> p (g c)"),
        in_=grouped[:].rearrange("p g c t -> p (g c t)"),
    )


def tile_instrumentedlocmblock_pb_t_kernel(
    tc, y_tilde, z_next, dt, glu_w1, glu_w2, glu_b1, glu_b2, out
):
    nc = tc.nc
    y_chunks = y_tilde.rearrange("(c q j) k -> c q j k", q=P, j=ROW_GROUPS)
    z_chunks = z_next.rearrange("(c q j) k -> c q j k", q=P, j=ROW_GROUPS)
    out_chunks = out.rearrange("(c q j) n -> c q j n", q=P, j=ROW_GROUPS)

    with ExitStack() as ctx:
        const = ctx.enter_context(tc.tile_pool(name="const", bufs=1))
        loads = ctx.enter_context(tc.tile_pool(name="loads", bufs=CHUNKS_IN_SBUF))
        work = ctx.enter_context(tc.tile_pool(name="work", bufs=2))
        turned_pool = ctx.enter_context(tc.psum_pool(name="turned", bufs=2))
        sums_pool = ctx.enter_context(tc.psum_pool(name="sums", bufs=2 * UNIT_TILES))
        back_pool = ctx.enter_context(tc.psum_pool(name="back", bufs=2))
        ctx.enter_context(tc.manual_schedule())

        loaded = {}
        grouped_of = {}

        def load(c):
            stacked = loads.tile([P, 2, MODES], BF16)
            for first_partition, chunks in ((0, y_chunks), (1, z_chunks)):
                nc.sync.dma_start(
                    out=stacked[first_partition:P:2, :, :],
                    in_=chunks[c][:, VECTOR_GROUPS, :].rearrange("(s r) k -> r s k", s=2),
                )
            y_rows = loads.tile([P, VECTOR_GROUPS, MODES], BF16)
            z_rows = loads.tile([P, VECTOR_GROUPS, MODES], BF16)
            for first, last in VECTOR_PIECES:
                nc.sync.dma_start(out=y_rows[:, first:last, :], in_=y_chunks[c][:, first:last, :])
                nc.sync.dma_start(out=z_rows[:, first:last, :], in_=z_chunks[c][:, first:last, :])
            loaded[c] = (y_rows, z_rows, stacked)

        def tensor_add(c):
            stacked = loaded[c][2]
            grouped = work.tile([P, PASSES, CHUNK_ROWS, 4], BF16, align_bytes=64)
            add_and_group(nc, turned_pool, one_and_dt, stacked, grouped, VECTOR_GROUPS)
            grouped_of[c] = grouped

        def vector_add_and_turn(c):
            y_rows, z_rows = loaded[c][0:2]
            y_next = work.tile([P, VECTOR_GROUPS, MODES], BF16)
            for first, last in VECTOR_PIECES:
                nc.vector.scalar_tensor_tensor(
                    out=y_next[:, first:last, :],
                    in0=z_rows[:, first:last, :],
                    scalar=dt_col[:, 0:1],
                    in1=y_rows[:, first:last, :],
                    op0=ALU.mult,
                    op1=ALU.add,
                )
                for j in range(first, last):
                    turn_and_group(
                        nc, turned_pool, ident, y_next[:].bitcast(F32), grouped_of[c][:].bitcast(F32), j
                    )

        def quantise_chunk(c):
            y_codes = work.tile([P, PASSES, CHUNK_ROWS], U32, align_bytes=64)
            y_scales = work.tile([P, PASSES, CHUNK_ROWS], U8, align_bytes=64)
            quantise(nc, grouped_of[c], y_codes, y_scales)
            return y_codes, y_scales

        def multiply(y_codes, y_scales):
            halves = []
            for h in range(UNIT_TILES):
                gate_sum = sums_pool.tile([P, CHUNK_ROWS], F32, tag="sum")
                value_sum = sums_pool.tile([P, CHUNK_ROWS], F32, tag="sum")
                for acc, unit_tile in ((gate_sum, h), (value_sum, UNIT_TILES + h)):
                    units = slice(unit_tile * P, (unit_tile + 1) * P)
                    for g in range(PASSES):
                        nc.tensor.matmul_mx(
                            out=acc[:],
                            lhsT=w_codes[:, g, units].bitcast(FP8X4),
                            lhsT_scale=w_scales[:, g, units],
                            rhs=y_codes[:, g, :].bitcast(FP8X4),
                            rhs_scale=y_scales[:, g, :],
                            start=(g == 0),
                            stop=(g == PASSES - 1),
                        )
                gate = work.tile([P, CHUNK_ROWS], F32, bufs=2 * UNIT_TILES)
                nc.scalar.activation(
                    out=gate[:], in_=gate_sum[:], func=ACT.Sigmoid, bias=bias_col[:, h : h + 1], scale=1.0
                )
                halves.append((gate, value_sum))
            return halves

        def gate_and_store(c, halves):
            product = work.tile([P, UNIT_TILES, CHUNK_ROWS], F32)
            backs = [
                back_pool.tile([P, 2, UNITS], F32, name="back%d" % pair, tag="back")
                for pair in range(ROW_GROUPS // 2)
            ]
            for h in range(UNIT_TILES):
                gate, value_sum = halves[h]
                nc.vector.scalar_tensor_tensor(
                    out=product[:, h, :],
                    in0=value_sum[:],
                    scalar=bias_col[:, UNIT_TILES + h : UNIT_TILES + h + 1],
                    in1=gate[:],
                    op0=ALU.add,
                    op1=ALU.mult,
                )
                for j in range(ROW_GROUPS):
                    nc.tensor.transpose(
                        backs[j // 2][:, j % 2, h * P : (h + 1) * P],
                        product[:, h, j * P : (j + 1) * P],
                        ident[:],
                    )
            result = work.tile([P, ROW_GROUPS, UNITS], F32)
            for pair in range(ROW_GROUPS // 2):
                groups = slice(2 * pair, 2 * pair + 2)
                nc.scalar.copy(out=result[:, groups, :], in_=backs[pair][:])
                nc.sync.dma_start(out=out_chunks[c][:, groups, :], in_=result[:, groups, :])

        ident = const.tile([P, P], F32)
        make_identity(nc, ident[:])

        dt_bf16 = const.tile([P, 1], BF16)
        nc.scalar.dma_start(out=dt_bf16[:], in_=dt.partition_broadcast(P))
        bias_bf16 = const.tile([2 * UNIT_TILES, P], BF16)
        nc.scalar.dma_start(
            out=bias_bf16[0:UNIT_TILES, :], in_=glu_b1.rearrange("(h n) -> h n", n=P)
        )
        nc.scalar.dma_start(
            out=bias_bf16[UNIT_TILES : 2 * UNIT_TILES, :], in_=glu_b2.rearrange("(h n) -> h n", n=P)
        )
        table_warmer = const.tile([P, 1], F32)
        nc.scalar.activation(out=table_warmer[:], in_=ident[:, 0:1], func=ACT.Sigmoid)

        w_rows = const.tile([P, 2 * UNIT_TILES, MODES], BF16)
        nc.sync.dma_start(
            out=w_rows[:, 0:UNIT_TILES, :], in_=glu_w1.rearrange("(h q) k -> q h k", q=P)
        )
        nc.sync.dma_start(
            out=w_rows[:, UNIT_TILES : 2 * UNIT_TILES, :], in_=glu_w2.rearrange("(h q) k -> q h k", q=P)
        )
        for c in range(CHUNKS_IN_SBUF):
            load(c)

        dt_col = const.tile([P, 1], F32)
        nc.vector.tensor_copy(out=dt_col[:], in_=dt_bf16[:])
        one_and_dt = const.tile([P, HALF], BF16)
        nc.vector.scalar_tensor_tensor(
            out=one_and_dt[:],
            in0=ident[:, 1:P:2],
            scalar=dt_col[:, 0:1],
            in1=ident[:, 0:P:2],
            op0=ALU.mult,
            op1=ALU.add,
        )

        bias_rows = const.tile([P, P], F32)
        nc.vector.memset(bias_rows[:], 0.0)
        nc.vector.tensor_copy(out=bias_rows[0 : 2 * UNIT_TILES, :], in_=bias_bf16[:])
        bias_turned = turned_pool.tile([P, PASSES, 2, P], F32, tag="turned")
        nc.tensor.transpose(bias_turned[:, 0, 0, :], bias_rows[:], ident[:])
        bias_col = const.tile([P, 2 * UNIT_TILES], F32)
        nc.scalar.copy(out=bias_col[:], in_=bias_turned[:, 0, 0, 0 : 2 * UNIT_TILES])

        w_grouped = const.tile([P, PASSES, CHUNK_ROWS, 4], BF16, align_bytes=64)
        for unit_tile in range(2 * UNIT_TILES):
            turn_and_group(
                nc, turned_pool, ident, w_rows[:].bitcast(F32), w_grouped[:].bitcast(F32), unit_tile
            )

        tensor_add(0)
        vector_add_and_turn(0)
        w_codes = const.tile([P, PASSES, CHUNK_ROWS], U32, align_bytes=64)
        w_scales = const.tile([P, PASSES, CHUNK_ROWS], U8, align_bytes=64)
        quantise(nc, w_grouped, w_codes, w_scales)

        for c in range(CHUNKS):
            if c + CHUNKS_IN_SBUF < CHUNKS:
                load(c + CHUNKS_IN_SBUF)
            y_codes, y_scales = quantise_chunk(c)
            if c + 1 < CHUNKS:
                tensor_add(c + 1)
            halves = multiply(y_codes, y_scales)
            if c + 1 < CHUNKS:
                vector_add_and_turn(c + 1)
            gate_and_store(c, halves)
